import numpy as np
import ml_dtypes


BF16 = ml_dtypes.bfloat16


def bf(x):
    return np.asarray(x, np.float32).astype(BF16)


def f64(x):
    return np.asarray(x).astype(np.float64)


E2M1 = np.array([0.0, 0.5, 1.0, 1.5, 2.0, 3.0, 4.0, 6.0, -0.0, -0.5, -1.0, -1.5, -2.0, -3.0, -4.0, -6.0])


def pack_weight(w, fmt):
    k, n = w.shape
    w = f64(bf(w)).reshape(k // 32, 32, n)
    amax = np.abs(w).max(1)
    if fmt == "e4m3":
        byte = np.frexp(amax)[1] - 1 + 127 - 7
    else:
        mant, ex = np.frexp(amax / 6.0)
        byte = np.where(mant > 0.5, ex, ex - 1) + 127
    byte = np.clip(np.where(amax > 0, byte, 1), 1, 254)
    scaled = (w * np.exp2(127.0 - byte)[:, None, :]).reshape(k, n).astype(np.float32)
    by_word = np.ascontiguousarray(scaled.reshape(k // 512, 128, 4, n).transpose(0, 1, 3, 2))
    if fmt == "e4m3":
        words = by_word.astype(ml_dtypes.float8_e4m3fn).view(np.uint8)
    else:
        c = by_word.astype(ml_dtypes.float4_e2m1fn).view(np.uint8) & 0xF
        words = c[..., 0::2] | (c[..., 1::2] << 4)
    return np.ascontiguousarray(words), np.ascontiguousarray(byte.astype(np.uint8).reshape(k // 512, 16, n))


def unpack_weight(words, scales, fmt):
    g, p, n, _ = words.shape
    if fmt == "e4m3":
        vals = np.ascontiguousarray(words).view(ml_dtypes.float8_e4m3fn).astype(np.float64)
    else:
        nib = np.empty((g, p, n, 4), np.uint8)
        nib[..., 0::2] = words & 0xF
        nib[..., 1::2] = words >> 4
        vals = E2M1[nib]
    vals = vals * np.repeat(np.exp2(scales.astype(np.float64) - 127.0), 8, axis=1)[..., None]
    return vals.transpose(0, 1, 3, 2).reshape(g * 512, n)

def pack4(w):
    words, scales = pack_weight(w, "e2m1")
    return words.reshape(words.shape[0], 128, -1), scales


def unpack4(words, scales):
    return unpack_weight(words.reshape(words.shape[0], 128, -1, 2), scales, "e2m1")


def kspread(k):
    return np.exp2(np.repeat(np.random.randint(-6, 7, k // 32), 32).astype(np.float64))


B, N, HID, H, D = 2, 256, 4096, 16, 32


def apply_rope(t, rope):
    freqs = rope[:, 0, :]
    cos = np.repeat(freqs[:, 0::2], 2, axis=-1)[None, None]
    sin = np.repeat(freqs[:, 1::2], 2, axis=-1)[None, None]
    tr = t.reshape(*t.shape[:-1], -1, 2)
    t_real, t_imag = tr[..., 0], tr[..., 1]
    t_rot = np.stack([-t_imag, t_real], axis=-1).reshape(t.shape)
    return t * cos + t_rot * sin


def setup_inputs():
    s = kspread(HID)
    x = np.random.standard_normal((B, N, HID)) * s
    x_words, x_scales = pack4(np.ascontiguousarray(x.reshape(B * N, HID).T))
    rope = bf(np.random.uniform(size=(N, 1, D)))
    words, scales = pack4(np.random.standard_normal((HID, 3 * H * D)) * 1.5 / np.sqrt(HID) / s[:, None])
    return {"x_words": x_words,
            "x_scales": x_scales,
            "rope": rope,
            "qkv_w_words": words,
            "qkv_w_scales": scales}


def reference(x_words, x_scales, rope, qkv_w_words, qkv_w_scales):
    r = f64(rope)
    xq = unpack4(x_words, x_scales).T.reshape(B, N, HID)
    qkv = (xq @ unpack4(qkv_w_words, qkv_w_scales)).reshape(B, N, 3, H, D)
    q = np.transpose(qkv[:, :, 0], (0, 2, 1, 3))
    k = np.transpose(qkv[:, :, 1], (0, 2, 1, 3))
    v = np.transpose(qkv[:, :, 2], (0, 2, 1, 3))
    return apply_rope(q, r), apply_rope(k, r), v

@@ -1,0 +1,183 @@
+from contextlib import ExitStack
+
+import concourse.mybir as mybir
+
+F32 = mybir.dt.float32
+BF16 = mybir.dt.bfloat16
+U8 = mybir.dt.uint8
+I32 = mybir.dt.int32
+FP4X4 = mybir.dt.float4_e2m1fn_x4
+MULT = mybir.AluOpType.mult
+ADD = mybir.AluOpType.add
+
+P = 128
+PASSES = 8
+TOKENS = 512
+HEADS = 16
+HEAD_DIM = 32
+BLOCK = HEADS * HEAD_DIM
+FLOPS = 2 * TOKENS * 4096 * 3 * BLOCK
+
+CODE_RUNS = ((0, 1), (1, 2), (2, 4), (4, 8))
+HALF_RUNS = ((0, 4), (4, 8))
+WARM = 7
+
+
+def tile_attention_pa_kernel(tc, x_words, x_scales, rope, qkv_w_words, qkv_w_scales, out_0, out_1, out_2):
+    nc = tc.nc
+    outs = (out_0, out_1, out_2)
+
+    with ExitStack() as ctx:
+        keep = ctx.enter_context(tc.tile_pool(name="keep", bufs=1))
+        work = ctx.enter_context(tc.tile_pool(name="work", bufs=3))
+        psum = ctx.enter_context(tc.psum_pool(name="psum", bufs=8))
+        ctx.enter_context(tc.manual_schedule())
+
+        zeros = keep.tile([P, BLOCK], BF16, name="zeros")
+        tiny = keep.tile([P, 8], F32, name="tiny")
+        x_planes = keep.tile([P, PASSES, TOKENS], U8, name="x_planes", align_bytes=64)
+        wq_planes = keep.tile([P, PASSES, BLOCK], U8, name="wq_planes", align_bytes=64)
+        wkv_planes = keep.tile([P, PASSES, 2 * BLOCK], U8, name="wkv_planes", align_bytes=64)
+        rope_sb = keep.tile([P, 2, HEAD_DIM], BF16, name="rope_sb")
+        cos_t = keep.tile([P, 2, HEAD_DIM], F32, name="cos_t")
+        sin_t = keep.tile([P, 2, HEAD_DIM], F32, name="sin_t")
+
+        nc.gpsimd.memset(zeros[:], 0.0)
+        nc.vector.memset(x_planes[:].bitcast(I32), 0)
+        nc.vector.memset(wq_planes[:].bitcast(I32), 0)
+        nc.gpsimd.dma_start(out=rope_sb[:], in_=rope.rearrange("(u p) o d -> p u (o d)", u=2))
+        nc.gpsimd.memset(wkv_planes[:].bitcast(F32), 0.0)
+        nc.scalar.copy(out=tiny[:], in_=zeros[:, 0:8])
+
+        x_of = {}
+        w_of = {}
+
+        def load_x(g0, g1):
+            t = keep.tile([P, g1 - g0, 2 * TOKENS], U8, name="x_codes%d" % g0, align_bytes=64)
+            nc.sync.dma_start(out=t[:].bitcast(I32), in_=x_words[g0:g1].rearrange("g p n -> p g n").bitcast(I32))
+            for g in range(g0, g1):
+                x_of[g] = t[:, g - g0, :]
+
+        def load_w(c, g0, g1):
+            t = keep.tile([P, g1 - g0, 2 * BLOCK], U8, name="w_codes%d_%d" % (c, g0), align_bytes=64)
+            nc.sync.dma_start(
+                out=t[:].bitcast(I32),
+                in_=qkv_w_words[g0:g1, :, 2 * BLOCK * c : 2 * BLOCK * (c + 1)].rearrange("g p n -> p g n").bitcast(I32),
+            )
+            for g in range(g0, g1):
+                w_of[(c, g)] = t[:, g - g0, :]
+
+        def load_planes(planes, scales):
+            for r in range(4):
+                nc.sync.dma_start(
+                    out=planes[r:P:32, :, :].bitcast(I32),
+                    in_=scales[:, r:16:4, :].rearrange("g q n -> q g n").bitcast(I32),
+                )
+
+        load_x(0, 1)
+        load_w(0, 0, 1)
+        load_planes(x_planes, x_scales)
+        load_planes(wq_planes, qkv_w_scales[:, :, 0:BLOCK])
+        for g0, g1 in CODE_RUNS[1:]:
+            load_x(g0, g1)
+            load_w(0, g0, g1)
+        load_planes(wkv_planes, qkv_w_scales[:, :, BLOCK : 3 * BLOCK])
+        for c in (1, 2):
+            for g0, g1 in HALF_RUNS:
+                load_w(c, g0, g1)
+
+        rope_v = rope_sb[:].rearrange("p u (j t) -> p (u j) t", t=2)
+        cos_v = cos_t[:].rearrange("p u (j t) -> p (u j) t", t=2)
+        sin_v = sin_t[:].rearrange("p u (j t) -> p (u j) t", t=2)
+        nc.gpsimd.tensor_copy(out=cos_v[:, :, 0:1], in_=rope_v[:, :, 0:1])
+        nc.gpsimd.tensor_copy(out=cos_v[:, :, 1:2], in_=rope_v[:, :, 0:1])
+        nc.gpsimd.tensor_copy(out=sin_v[:, :, 0:1], in_=rope_v[:, :, 1:2])
+        nc.gpsimd.tensor_scalar(out=sin_v[:, :, 1:2], in0=rope_v[:, :, 1:2], scalar1=-1.0, scalar2=0.0, op0=MULT, op1=ADD)
+
+        warm = psum.tile([P, BLOCK], F32, name="warm", tag="acc")
+        for n in range(WARM):
+            nc.tensor.matmul(out=warm[:], lhsT=zeros[:, 0:P], rhs=zeros[:], start=True, stop=True)
+
+        def w_plane(c, g, n0, n1):
+            if c == 0:
+                return wq_planes[:, g, n0:n1]
+            return wkv_planes[:, g, BLOCK * (c - 1) + n0 : BLOCK * (c - 1) + n1]
+
+        def mm(acc, i, c, g, n0, n1):
+            nc.tensor.matmul_mx(
+                out=acc,
+                lhsT=x_of[g][:, 2 * P * i : 2 * P * (i + 1)].bitcast(FP4X4),
+                lhsT_scale=x_planes[:, g, P * i : P * (i + 1)],
+                rhs=w_of[(c, g)][:, 2 * n0 : 2 * n1].bitcast(FP4X4),
+                rhs_scale=w_plane(c, g, n0, n1),
+                start=(g == 0),
+                stop=(g == PASSES - 1),
+            )
+
+        def out_view(c, i, h0, h1):
+            b, u = divmod(i, 2)
+            return outs[c][b, h0:h1, P * u : P * (u + 1), :].rearrange("h p d -> p h d")
+
+        banks = []
+        for i in range(4):
+            acc = psum.tile([P, BLOCK], F32, name="acc_q%d" % i, tag="acc")
+            banks.append((0, i, acc))
+        for g in range(PASSES):
+            for c, i, acc in banks:
+                mm(acc[:], i, c, g, 0, BLOCK)
+        for i in range(4):
+            acc = psum.tile([P, BLOCK], F32, name="acc_k%d" % i, tag="acc")
+            banks.append((1, i, acc))
+            for g in range(PASSES):
+                mm(acc[:], i, 1, g, 0, BLOCK)
+
+        parts = {}
+
+        def rope_mul(n):
+            c, i, acc = banks[n]
+            u = i % 2
+            t1 = work.tile([P, BLOCK], F32, name="t1", tag="t1")
+            t2 = work.tile([P, BLOCK], F32, name="t2", tag="t2")
+            acc_v = acc[:].rearrange("p (h d) -> p h d", h=HEADS)
+            nc.vector.tensor_tensor(
+                out=t1[:].rearrange("p (h d) -> p h d", h=HEADS), in0=acc_v,
+                in1=cos_t[:, u, :].unsqueeze(1).to_broadcast([P, HEADS, HEAD_DIM]), op=MULT)
+            nc.vector.tensor_tensor(
+                out=t2[:].rearrange("p (h d) -> p h d", h=HEADS), in0=acc_v,
+                in1=sin_t[:, u, :].unsqueeze(1).to_broadcast([P, HEADS, HEAD_DIM]), op=MULT)
+            parts[n] = (t1, t2)
+
+        def rope_add(n):
+            c, i, acc = banks[n]
+            t1, t2 = parts[n]
+            res = keep.tile([P, BLOCK], F32, name="res%d_%d" % (c, i))
+            nc.vector.tensor_tensor(
+                out=res[:].rearrange("p (x t) -> p x t", t=2),
+                in0=t1[:].rearrange("p (x t) -> p x t", t=2),
+                in1=t2[:].rearrange("p (x t) -> p x t", t=2)[:, :, ::-1],
+                op=ADD)
+            nc.sync.dma_start(out=out_view(c, i, 0, HEADS), in_=res[:].rearrange("p (h d) -> p h d", h=HEADS))
+
+        rope_mul(0)
+        for n in range(1, len(banks)):
+            rope_mul(n)
+            rope_add(n - 1)
+        rope_add(len(banks) - 1)
+
+        for i in range(3):
+            acc = psum.tile([P, BLOCK], F32, name="acc_v%d" % i, tag="acc")
+            for g in range(PASSES):
+                mm(acc[:], i, 2, g, 0, BLOCK)
+            res = keep.tile([P, BLOCK], F32, name="res2_%d" % i)
+            nc.scalar.copy(out=res[:], in_=acc[:])
+            nc.scalar.dma_start(out=out_view(2, i, 0, HEADS), in_=res[:].rearrange("p (h d) -> p h d", h=HEADS))
+        half = BLOCK // 2
+        for s in range(2):
+            acc = psum.tile([P, BLOCK], F32, name="acc_v3_%d" % s, tag="acc")
+            for g in range(PASSES):
+                mm(acc[:, 0:half], 3, 2, g, half * s, half * (s + 1))
+            res = keep.tile([P, half], F32, name="res2_3_%d" % s)
+            nc.scalar.copy(out=res[:], in_=acc[:, 0:half])
+            nc.scalar.dma_start(
+                out=out_view(2, 3, HEADS // 2 * s, HEADS // 2 * (s + 1)),
+                in_=res[:].rearrange("p (h d) -> p h d", d=HEAD_DIM))

@@ -19,6 +19,7 @@ BLOCK = HEADS * HEAD_DIM
 FLOPS = 2 * TOKENS * 4096 * 3 * BLOCK
 
 CODE_RUNS = ((0, 1), (1, 2), (2, 4), (4, 8))
+PLANE_RUNS = ((0, 2), (2, 4), (4, 8))
 HALF_RUNS = ((0, 4), (4, 8))
 WARM = 7
 
@@ -35,7 +36,7 @@ def tile_attention_pa_kernel(tc, x_words, x_scales, rope, qkv_w_words, qkv_w_sca
 
         zeros = keep.tile([P, BLOCK], BF16, name="zeros")
         tiny = keep.tile([P, 8], F32, name="tiny")
-        x_planes = keep.tile([P, PASSES, TOKENS], U8, name="x_planes", align_bytes=64)
+        xs_raw = keep.tile([P, PASSES, TOKENS], U8, name="xs_raw", align_bytes=64)
         wq_planes = keep.tile([P, PASSES, BLOCK], U8, name="wq_planes", align_bytes=64)
         wkv_planes = keep.tile([P, PASSES, 2 * BLOCK], U8, name="wkv_planes", align_bytes=64)
         rope_sb = keep.tile([P, 2, HEAD_DIM], BF16, name="rope_sb")
@@ -43,20 +44,22 @@ def tile_attention_pa_kernel(tc, x_words, x_scales, rope, qkv_w_words, qkv_w_sca
         sin_t = keep.tile([P, 2, HEAD_DIM], F32, name="sin_t")
 
         nc.gpsimd.memset(zeros[:], 0.0)
-        nc.vector.memset(x_planes[:].bitcast(I32), 0)
+        nc.vector.memset(xs_raw[:].bitcast(I32), 0)
         nc.vector.memset(wq_planes[:].bitcast(I32), 0)
-        nc.gpsimd.dma_start(out=rope_sb[:], in_=rope.rearrange("(u p) o d -> p u (o d)", u=2))
+        nc.gpsimd.dma_start(out=rope_sb[:], in_=rope.rearrange("(m j) o d -> m j (o d)", j=2))
         nc.gpsimd.memset(wkv_planes[:].bitcast(F32), 0.0)
         nc.scalar.copy(out=tiny[:], in_=zeros[:, 0:8])
 
+        raw_of = {}
         x_of = {}
+        xp_of = {}
         w_of = {}
 
         def load_x(g0, g1):
-            t = keep.tile([P, g1 - g0, 2 * TOKENS], U8, name="x_codes%d" % g0, align_bytes=64)
+            t = keep.tile([P, g1 - g0, 2 * TOKENS], U8, name="x_raw%d" % g0, align_bytes=64)
             nc.sync.dma_start(out=t[:].bitcast(I32), in_=x_words[g0:g1].rearrange("g p n -> p g n").bitcast(I32))
             for g in range(g0, g1):
-                x_of[g] = t[:, g - g0, :]
+                raw_of[g] = t[:, g - g0, :]
 
         def load_w(c, g0, g1):
             t = keep.tile([P, g1 - g0, 2 * BLOCK], U8, name="w_codes%d_%d" % (c, g0), align_bytes=64)
@@ -75,8 +78,8 @@ def tile_attention_pa_kernel(tc, x_words, x_scales, rope, qkv_w_words, qkv_w_sca
                 )
 
         load_x(0, 1)
+        load_planes(xs_raw, x_scales)
         load_w(0, 0, 1)
-        load_planes(x_planes, x_scales)
         load_planes(wq_planes, qkv_w_scales[:, :, 0:BLOCK])
         for g0, g1 in CODE_RUNS[1:]:
             load_x(g0, g1)
@@ -85,6 +88,33 @@ def tile_attention_pa_kernel(tc, x_words, x_scales, rope, qkv_w_words, qkv_w_sca
         for c in (1, 2):
             for g0, g1 in HALF_RUNS:
                 load_w(c, g0, g1)
+
+        def sort_codes(g):
+            t = keep.tile([P, 2 * TOKENS], U8, name="x_codes%d" % g, align_bytes=64)
+            nc.vector.tensor_copy(
+                out=t[:].rearrange("p (j m e) -> p j m e", j=2, e=2),
+                in_=raw_of[g].rearrange("p (m j e) -> p j m e", j=2, e=2),
+            )
+            x_of[g] = t
+
+        def sort_planes(g0, g1):
+            t = keep.tile([P, g1 - g0, TOKENS], U8, name="x_planes%d" % g0, align_bytes=64)
+            nc.vector.tensor_copy(
+                out=t[:].rearrange("p g (j m) -> p g j m", j=2),
+                in_=xs_raw[:, g0:g1, :].rearrange("p g (m j) -> p g j m", j=2),
+            )
+            for g in range(g0, g1):
+                xp_of[g] = t[:, g - g0, :]
+
+        sort_codes(0)
+        sort_planes(0, 2)
+        sort_codes(1)
+        sort_planes(2, 4)
+        sort_codes(2)
+        sort_codes(3)
+        sort_planes(4, 8)
+        for g in range(4, PASSES):
+            sort_codes(g)
 
         rope_v = rope_sb[:].rearrange("p u (j t) -> p (u j) t", t=2)
         cos_v = cos_t[:].rearrange("p u (j t) -> p (u j) t", t=2)
@@ -103,60 +133,68 @@ def tile_attention_pa_kernel(tc, x_words, x_scales, rope, qkv_w_words, qkv_w_sca
                 return wq_planes[:, g, n0:n1]
             return wkv_planes[:, g, BLOCK * (c - 1) + n0 : BLOCK * (c - 1) + n1]
 
-        def mm(acc, i, c, g, n0, n1):
+        def mm(acc, b, j, c, g, n0, n1):
+            i = 2 * j + b
             nc.tensor.matmul_mx(
                 out=acc,
                 lhsT=x_of[g][:, 2 * P * i : 2 * P * (i + 1)].bitcast(FP4X4),
-                lhsT_scale=x_planes[:, g, P * i : P * (i + 1)],
+                lhsT_scale=xp_of[g][:, P * i : P * (i + 1)],
                 rhs=w_of[(c, g)][:, 2 * n0 : 2 * n1].bitcast(FP4X4),
                 rhs_scale=w_plane(c, g, n0, n1),
                 start=(g == 0),
                 stop=(g == PASSES - 1),
             )
 
-        def out_view(c, i, h0, h1):
-            b, u = divmod(i, 2)
-            return outs[c][b, h0:h1, P * u : P * (u + 1), :].rearrange("h p d -> p h d")
+        def store(queue, c, b, h0, h1, res):
+            queue.dma_start(
+                out=outs[c][b, h0:h1, :, :].rearrange("h (m j) d -> m h (j d)", j=2),
+                in_=res[:].rearrange("p h j d -> p h (j d)"),
+            )
 
         banks = []
-        for i in range(4):
-            acc = psum.tile([P, BLOCK], F32, name="acc_q%d" % i, tag="acc")
-            banks.append((0, i, acc))
+        for b in range(2):
+            for j in range(2):
+                acc = psum.tile([P, BLOCK], F32, name="acc_q%d%d" % (b, j), tag="acc")
+                banks.append((0, b, j, acc))
         for g in range(PASSES):
-            for c, i, acc in banks:
-                mm(acc[:], i, c, g, 0, BLOCK)
-        for i in range(4):
-            acc = psum.tile([P, BLOCK], F32, name="acc_k%d" % i, tag="acc")
-            banks.append((1, i, acc))
-            for g in range(PASSES):
-                mm(acc[:], i, 1, g, 0, BLOCK)
+            for c, b, j, acc in banks:
+                mm(acc[:], b, j, c, g, 0, BLOCK)
+        for b in range(2):
+            for j in range(2):
+                acc = psum.tile([P, BLOCK], F32, name="acc_k%d%d" % (b, j), tag="acc")
+                banks.append((1, b, j, acc))
+                for g in range(PASSES):
+                    mm(acc[:], b, j, 1, g, 0, BLOCK)
 
         parts = {}
+        res_of = {}
 
         def rope_mul(n):
-            c, i, acc = banks[n]
-            u = i % 2
+            c, b, j, acc = banks[n]
             t1 = work.tile([P, BLOCK], F32, name="t1", tag="t1")
             t2 = work.tile([P, BLOCK], F32, name="t2", tag="t2")
             acc_v = acc[:].rearrange("p (h d) -> p h d", h=HEADS)
             nc.vector.tensor_tensor(
                 out=t1[:].rearrange("p (h d) -> p h d", h=HEADS), in0=acc_v,
-                in1=cos_t[:, u, :].unsqueeze(1).to_broadcast([P, HEADS, HEAD_DIM]), op=MULT)
+                in1=cos_t[:, j, :].unsqueeze(1).to_broadcast([P, HEADS, HEAD_DIM]), op=MULT)
             nc.vector.tensor_tensor(
                 out=t2[:].rearrange("p (h d) -> p h d", h=HEADS), in0=acc_v,
-                in1=sin_t[:, u, :].unsqueeze(1).to_broadcast([P, HEADS, HEAD_DIM]), op=MULT)
+                in1=sin_t[:, j, :].unsqueeze(1).to_broadcast([P, HEADS, HEAD_DIM]), op=MULT)
             parts[n] = (t1, t2)
 
         def rope_add(n):
-            c, i, acc = banks[n]
+            c, b, j, acc = banks[n]
             t1, t2 = parts[n]
-            res = keep.tile([P, BLOCK], F32, name="res%d_%d" % (c, i))
+            if j == 0:
+                res_of[(c, b)] = keep.tile([P, HEADS, 2, HEAD_DIM], F32, name="res%d_%d" % (c, b))
+            res = res_of[(c, b)]
             nc.vector.tensor_tensor(
-                out=res[:].rearrange("p (x t) -> p x t", t=2),
-                in0=t1[:].rearrange("p (x t) -> p x t", t=2),
-                in1=t2[:].rearrange("p (x t) -> p x t", t=2)[:, :, ::-1],
+                out=res[:, :, j, :].rearrange("p h (x t) -> p h x t", t=2),
+                in0=t1[:].rearrange("p (h x t) -> p h x t", h=HEADS, t=2),
+                in1=t2[:].rearrange("p (h x t) -> p h x t", h=HEADS, t=2)[:, :, :, ::-1],
                 op=ADD)
-            nc.sync.dma_start(out=out_view(c, i, 0, HEADS), in_=res[:].rearrange("p (h d) -> p h d", h=HEADS))
+            if j == 1:
+                store(nc.sync, c, b, 0, HEADS, res)
 
         rope_mul(0)
         for n in range(1, len(banks)):
@@ -164,20 +202,20 @@ def tile_attention_pa_kernel(tc, x_words, x_scales, rope, qkv_w_words, qkv_w_sca
             rope_add(n - 1)
         rope_add(len(banks) - 1)
 
-        for i in range(3):
-            acc = psum.tile([P, BLOCK], F32, name="acc_v%d" % i, tag="acc")
+        res = keep.tile([P, HEADS, 2, HEAD_DIM], F32, name="res2_0")
+        for j in range(2):
+            acc = psum.tile([P, BLOCK], F32, name="acc_v0%d" % j, tag="acc")
             for g in range(PASSES):
-                mm(acc[:], i, 2, g, 0, BLOCK)
-            res = keep.tile([P, BLOCK], F32, name="res2_%d" % i)
-            nc.scalar.copy(out=res[:], in_=acc[:])
-            nc.scalar.dma_start(out=out_view(2, i, 0, HEADS), in_=res[:].rearrange("p (h d) -> p h d", h=HEADS))
+                mm(acc[:], 0, j, 2, g, 0, BLOCK)
+            nc.scalar.copy(out=res[:, :, j, :], in_=acc[:].rearrange("p (h d) -> p h d", h=HEADS))
+        store(nc.scalar, 2, 0, 0, HEADS, res)
         half = BLOCK // 2
+        hh = HEADS // 2
         for s in range(2):
-            acc = psum.tile([P, BLOCK], F32, name="acc_v3_%d" % s, tag="acc")
-            for g in range(PASSES):
-                mm(acc[:, 0:half], 3, 2, g, half * s, half * (s + 1))
-            res = keep.tile([P, half], F32, name="res2_3_%d" % s)
-            nc.scalar.copy(out=res[:], in_=acc[:, 0:half])
-            nc.scalar.dma_start(
-                out=out_view(2, 3, HEADS // 2 * s, HEADS // 2 * (s + 1)),
-                in_=res[:].rearrange("p (h d) -> p h d", d=HEAD_DIM))
+            res = keep.tile([P, hh, 2, HEAD_DIM], F32, name="res2_1_%d" % s)
+            for j in range(2):
+                acc = psum.tile([P, BLOCK], F32, name="acc_v1%d%d" % (s, j), tag="acc")
+                for g in range(PASSES):
+                    mm(acc[:, 0:half], 1, j, 2, g, half * s, half * (s + 1))
+                nc.scalar.copy(out=res[:, :, j, :], in_=acc[:, 0:half].rearrange("p (h d) -> p h d", h=hh))
+            store(nc.scalar, 2, 1, hh * s, hh * (s + 1), res)

@@ -18,10 +18,8 @@ HEAD_DIM = 32
 BLOCK = HEADS * HEAD_DIM
 FLOPS = 2 * TOKENS * 4096 * 3 * BLOCK
 
-CODE_RUNS = ((0, 1), (1, 2), (2, 4), (4, 8))
-PLANE_RUNS = ((0, 2), (2, 4), (4, 8))
-HALF_RUNS = ((0, 4), (4, 8))
-WARM = 7
+K_SWEEP = 4
+WARM = 10
 
 
 def tile_attention_pa_kernel(tc, x_words, x_scales, rope, qkv_w_words, qkv_w_scales, out_0, out_1, out_2):
@@ -36,24 +34,36 @@ def tile_attention_pa_kernel(tc, x_words, x_scales, rope, qkv_w_words, qkv_w_sca
 
         zeros = keep.tile([P, BLOCK], BF16, name="zeros")
         tiny = keep.tile([P, 8], F32, name="tiny")
-        xs_raw = keep.tile([P, PASSES, TOKENS], U8, name="xs_raw", align_bytes=64)
-        wq_planes = keep.tile([P, PASSES, BLOCK], U8, name="wq_planes", align_bytes=64)
-        wkv_planes = keep.tile([P, PASSES, 2 * BLOCK], U8, name="wkv_planes", align_bytes=64)
-        rope_sb = keep.tile([P, 2, HEAD_DIM], BF16, name="rope_sb")
-        cos_t = keep.tile([P, 2, HEAD_DIM], F32, name="cos_t")
-        sin_t = keep.tile([P, 2, HEAD_DIM], F32, name="sin_t")
-
-        nc.gpsimd.memset(zeros[:], 0.0)
-        nc.vector.memset(xs_raw[:].bitcast(I32), 0)
-        nc.vector.memset(wq_planes[:].bitcast(I32), 0)
-        nc.gpsimd.dma_start(out=rope_sb[:], in_=rope.rearrange("(m j) o d -> m j (o d)", j=2))
-        nc.gpsimd.memset(wkv_planes[:].bitcast(F32), 0.0)
-        nc.scalar.copy(out=tiny[:], in_=zeros[:, 0:8])
+        rope_sb = keep.tile([P, 6, HEAD_DIM], BF16, name="rope_sb")
+        cos_t = keep.tile([P, 6, HEAD_DIM], F32, name="cos_t")
+        sin_t = keep.tile([P, 6, HEAD_DIM], F32, name="sin_t")
 
         raw_of = {}
+        rawp_of = {}
         x_of = {}
         xp_of = {}
         w_of = {}
+        wp_of = {}
+
+        def plane_tile(name, n, engine):
+            t = keep.tile([P, n, BLOCK], U8, name=name, align_bytes=64)
+            if engine == 0:
+                nc.vector.memset(t[:].bitcast(I32), 0)
+            else:
+                nc.gpsimd.memset(t[:].bitcast(F32), 0.0)
+            return t
+
+        xs_a = plane_tile("xs_a", 4, 0)
+        qs_a = plane_tile("qs_a", 4, 0)
+        nc.vector.memset(zeros[:], 0.0)
+        xs_b = plane_tile("xs_b", 4, 0)
+        qs_b = plane_tile("qs_b", 4, 0)
+        nc.gpsimd.dma_start(out=rope_sb[:, 0:2, :], in_=rope.rearrange("(u p) o d -> p u (o d)", u=2))
+        for b in range(2):
+            nc.gpsimd.dma_start(out=rope_sb[b:P:2, 2:6, :], in_=rope.rearrange("(q j) o d -> q j (o d)", j=4))
+        ks = plane_tile("ks", 8, 1)
+        vs = plane_tile("vs", 8, 1)
+        nc.scalar.copy(out=tiny[:], in_=zeros[:, 0:8])
 
         def load_x(g0, g1):
             t = keep.tile([P, g1 - g0, 2 * TOKENS], U8, name="x_raw%d" % g0, align_bytes=64)
@@ -70,55 +80,68 @@ def tile_attention_pa_kernel(tc, x_words, x_scales, rope, qkv_w_words, qkv_w_sca
             for g in range(g0, g1):
                 w_of[(c, g)] = t[:, g - g0, :]
 
-        def load_planes(planes, scales):
+        def load_planes(planes, scales, g0, g1):
             for r in range(4):
                 nc.sync.dma_start(
                     out=planes[r:P:32, :, :].bitcast(I32),
-                    in_=scales[:, r:16:4, :].rearrange("g q n -> q g n").bitcast(I32),
+                    in_=scales[g0:g1, r:16:4, :].rearrange("g q n -> q g n").bitcast(I32),
                 )
 
+        def load_xs(planes, g0, g1):
+            load_planes(planes, x_scales, g0, g1)
+            for g in range(g0, g1):
+                rawp_of[g] = planes[:, g - g0, :]
+
+        def load_ws(planes, c, g0, g1):
+            load_planes(planes, qkv_w_scales[:, :, BLOCK * c : BLOCK * (c + 1)], g0, g1)
+            for g in range(g0, g1):
+                wp_of[(c, g)] = planes[:, g - g0, :]
+
         load_x(0, 1)
-        load_planes(xs_raw, x_scales)
         load_w(0, 0, 1)
-        load_planes(wq_planes, qkv_w_scales[:, :, 0:BLOCK])
-        for g0, g1 in CODE_RUNS[1:]:
-            load_x(g0, g1)
-            load_w(0, g0, g1)
-        load_planes(wkv_planes, qkv_w_scales[:, :, BLOCK : 3 * BLOCK])
-        for c in (1, 2):
-            for g0, g1 in HALF_RUNS:
-                load_w(c, g0, g1)
+        load_xs(xs_a, 0, 4)
+        load_ws(qs_a, 0, 0, 4)
+        load_x(1, 2)
+        load_w(0, 1, 2)
+        load_x(2, 4)
+        load_w(0, 2, 4)
+        load_xs(xs_b, 4, 8)
+        load_ws(qs_b, 0, 4, 8)
+        load_x(4, 6)
+        load_w(0, 4, 6)
+        load_x(6, 8)
+        load_w(0, 6, 8)
+        load_ws(ks, 1, 0, 8)
+        load_w(1, 0, 2)
+        load_w(1, 2, 4)
+        load_w(1, 4, 8)
+        load_ws(vs, 2, 0, 8)
+        load_w(2, 0, 4)
+        load_w(2, 4, 8)
 
         def sort_codes(g):
             t = keep.tile([P, 2 * TOKENS], U8, name="x_codes%d" % g, align_bytes=64)
             nc.vector.tensor_copy(
-                out=t[:].rearrange("p (j m e) -> p j m e", j=2, e=2),
-                in_=raw_of[g].rearrange("p (m j e) -> p j m e", j=2, e=2),
+                out=t[:].rearrange("p (j q b e) -> p j q b e", j=4, b=2, e=2),
+                in_=raw_of[g].rearrange("p (b q j e) -> p j q b e", b=2, j=4, e=2),
             )
             x_of[g] = t
 
-        def sort_planes(g0, g1):
-            t = keep.tile([P, g1 - g0, TOKENS], U8, name="x_planes%d" % g0, align_bytes=64)
+        def sort_plane(g):
+            t = keep.tile([P, TOKENS], U8, name="x_plane%d" % g, align_bytes=64)
             nc.vector.tensor_copy(
-                out=t[:].rearrange("p g (j m) -> p g j m", j=2),
-                in_=xs_raw[:, g0:g1, :].rearrange("p g (m j) -> p g j m", j=2),
+                out=t[:].rearrange("p (j q b) -> p j q b", j=4, b=2),
+                in_=rawp_of[g].rearrange("p (b q j) -> p j q b", b=2, j=4),
             )
-            for g in range(g0, g1):
-                xp_of[g] = t[:, g - g0, :]
+            xp_of[g] = t
 
-        sort_codes(0)
-        sort_planes(0, 2)
-        sort_codes(1)
-        sort_planes(2, 4)
-        sort_codes(2)
-        sort_codes(3)
-        sort_planes(4, 8)
-        for g in range(4, PASSES):
+        for g in range(PASSES):
             sort_codes(g)
+            sort_plane(g)
 
-        rope_v = rope_sb[:].rearrange("p u (j t) -> p (u j) t", t=2)
-        cos_v = cos_t[:].rearrange("p u (j t) -> p (u j) t", t=2)
-        sin_v = sin_t[:].rearrange("p u (j t) -> p (u j) t", t=2)
+        rope_v = rope_sb[:].rearrange("p u (i t) -> p (u i) t", t=2)
+        cos_v = cos_t[:].rearrange("p u (i t) -> p (u i) t", t=2)
+        sin_v = sin_t[:].rearrange("p u (i t) -> p (u i) t", t=2)
         nc.gpsimd.tensor_copy(out=cos_v[:, :, 0:1], in_=rope_v[:, :, 0:1])
         nc.gpsimd.tensor_copy(out=cos_v[:, :, 1:2], in_=rope_v[:, :, 0:1])
         nc.gpsimd.tensor_copy(out=sin_v[:, :, 0:1], in_=rope_v[:, :, 1:2])
@@ -128,94 +151,95 @@ def tile_attention_pa_kernel(tc, x_words, x_scales, rope, qkv_w_words, qkv_w_sca
         for n in range(WARM):
             nc.tensor.matmul(out=warm[:], lhsT=zeros[:, 0:P], rhs=zeros[:], start=True, stop=True)
 
-        def w_plane(c, g, n0, n1):
-            if c == 0:
-                return wq_planes[:, g, n0:n1]
-            return wkv_planes[:, g, BLOCK * (c - 1) + n0 : BLOCK * (c - 1) + n1]
-
-        def mm(acc, b, j, c, g, n0, n1):
-            i = 2 * j + b
+        def mm(acc, codes, plane, i, c, g, n0, n1):
             nc.tensor.matmul_mx(
                 out=acc,
-                lhsT=x_of[g][:, 2 * P * i : 2 * P * (i + 1)].bitcast(FP4X4),
-                lhsT_scale=xp_of[g][:, P * i : P * (i + 1)],
+                lhsT=codes[:, 2 * P * i : 2 * P * (i + 1)].bitcast(FP4X4),
+                lhsT_scale=plane[:, P * i : P * (i + 1)],
                 rhs=w_of[(c, g)][:, 2 * n0 : 2 * n1].bitcast(FP4X4),
-                rhs_scale=w_plane(c, g, n0, n1),
+                rhs_scale=wp_of[(c, g)][:, n0:n1],
                 start=(g == 0),
                 stop=(g == PASSES - 1),
             )
 
-        def store(queue, c, b, h0, h1, res):
-            queue.dma_start(
-                out=outs[c][b, h0:h1, :, :].rearrange("h (m j) d -> m h (j d)", j=2),
-                in_=res[:].rearrange("p h j d -> p h (j d)"),
-            )
+        def mm_plain(acc, i, c, g):
+            mm(acc, raw_of[g], rawp_of[g], i, c, g, 0, BLOCK)
 
-        banks = []
-        for b in range(2):
-            for j in range(2):
-                acc = psum.tile([P, BLOCK], F32, name="acc_q%d%d" % (b, j), tag="acc")
-                banks.append((0, b, j, acc))
+        def mm_sorted(acc, j, c, g, n0, n1):
+            mm(acc, x_of[g], xp_of[g], j, c, g, n0, n1)
+
+        q_banks = []
+        for i in range(4):
+            acc = psum.tile([P, BLOCK], F32, name="acc_q%d" % i, tag="acc")
+            q_banks.append(acc)
         for g in range(PASSES):
-            for c, b, j, acc in banks:
-                mm(acc[:], b, j, c, g, 0, BLOCK)
-        for b in range(2):
-            for j in range(2):
-                acc = psum.tile([P, BLOCK], F32, name="acc_k%d%d" % (b, j), tag="acc")
-                banks.append((1, b, j, acc))
-                for g in range(PASSES):
-                    mm(acc[:], b, j, 1, g, 0, BLOCK)
+            for i in range(4):
+                mm_plain(q_banks[i][:], i, 0, g)
+        k_banks = []
+        for j in range(4):
+            acc = psum.tile([P, BLOCK], F32, name="acc_k%d" % j, tag="acc")
+            k_banks.append(acc)
+        for g in range(K_SWEEP):
+            for j in range(4):
+                mm_sorted(k_banks[j][:], j, 1, g, 0, BLOCK)
+        for j in range(4):
+            for g in range(K_SWEEP, PASSES):
+                mm_sorted(k_banks[j][:], j, 1, g, 0, BLOCK)
 
+        def store_sorted(queues, c, h0, h1, res):
+            for b in range(2):
+                queues[b].dma_start(
+                    out=outs[c][b, h0:h1, :, :].rearrange("h (q j) d -> q h (j d)", j=4),
+                    in_=res[b:P:2, :, :, :].rearrange("p h j d -> p h (j d)"),
+                )
+
+        res_k = keep.tile([P, HEADS, 4, HEAD_DIM], F32, name="res_k")
         parts = {}
-        res_of = {}
 
         def rope_mul(n):
-            c, b, j, acc = banks[n]
+            acc, slot = (q_banks[n], n % 2) if n < 4 else (k_banks[n - 4], n - 2)
             t1 = work.tile([P, BLOCK], F32, name="t1", tag="t1")
             t2 = work.tile([P, BLOCK], F32, name="t2", tag="t2")
             acc_v = acc[:].rearrange("p (h d) -> p h d", h=HEADS)
             nc.vector.tensor_tensor(
                 out=t1[:].rearrange("p (h d) -> p h d", h=HEADS), in0=acc_v,
-                in1=cos_t[:, j, :].unsqueeze(1).to_broadcast([P, HEADS, HEAD_DIM]), op=MULT)
+                in1=cos_t[:, slot, :].unsqueeze(1).to_broadcast([P, HEADS, HEAD_DIM]), op=MULT)
             nc.vector.tensor_tensor(
                 out=t2[:].rearrange("p (h d) -> p h d", h=HEADS), in0=acc_v,
-                in1=sin_t[:, j, :].unsqueeze(1).to_broadcast([P, HEADS, HEAD_DIM]), op=MULT)
+                in1=sin_t[:, slot, :].unsqueeze(1).to_broadcast([P, HEADS, HEAD_DIM]), op=MULT)
             parts[n] = (t1, t2)
 
         def rope_add(n):
-            c, b, j, acc = banks[n]
             t1, t2 = parts[n]
-            if j == 0:
-                res_of[(c, b)] = keep.tile([P, HEADS, 2, HEAD_DIM], F32, name="res%d_%d" % (c, b))
-            res = res_of[(c, b)]
+            if n < 4:
+                res = keep.tile([P, HEADS, HEAD_DIM], F32, name="res_q%d" % n)
+                dst = res[:]
+            else:
+                dst = res_k[:, :, n - 4, :]
             nc.vector.tensor_tensor(
-                out=res[:, :, j, :].rearrange("p h (x t) -> p h x t", t=2),
+                out=dst.rearrange("p h (x t) -> p h x t", t=2),
                 in0=t1[:].rearrange("p (h x t) -> p h x t", h=HEADS, t=2),
                 in1=t2[:].rearrange("p (h x t) -> p h x t", h=HEADS, t=2)[:, :, :, ::-1],
                 op=ADD)
-            if j == 1:
-                store(nc.sync, c, b, 0, HEADS, res)
+            if n < 4:
+                b, u = divmod(n, 2)
+                nc.sync.dma_start(out=outs[0][b, :, P * u : P * (u + 1), :].rearrange("h p d -> p h d"), in_=res[:])
+            if n == 7:
+                store_sorted((nc.sync, nc.sync), 1, 0, HEADS, res_k)
 
         rope_mul(0)
-        for n in range(1, len(banks)):
+        for n in range(1, 8):
             rope_mul(n)
             rope_add(n - 1)
-        rope_add(len(banks) - 1)
+        rope_add(7)
 
-        res = keep.tile([P, HEADS, 2, HEAD_DIM], F32, name="res2_0")
-        for j in range(2):
-            acc = psum.tile([P, BLOCK], F32, name="acc_v0%d" % j, tag="acc")
-            for g in range(PASSES):
-                mm(acc[:], 0, j, 2, g, 0, BLOCK)
-            nc.scalar.copy(out=res[:, :, j, :], in_=acc[:].rearrange("p (h d) -> p h d", h=HEADS))
-        store(nc.scalar, 2, 0, 0, HEADS, res)
         half = BLOCK // 2
         hh = HEADS // 2
         for s in range(2):
-            res = keep.tile([P, hh, 2, HEAD_DIM], F32, name="res2_1_%d" % s)
-            for j in range(2):
-                acc = psum.tile([P, BLOCK], F32, name="acc_v1%d%d" % (s, j), tag="acc")
+            res = keep.tile([P, hh, 4, HEAD_DIM], F32, name="res_v%d" % s)
+            for j in range(4):
+                acc = psum.tile([P, BLOCK], F32, name="acc_v%d%d" % (s, j), tag="acc")
                 for g in range(PASSES):
-                    mm(acc[:, 0:half], 1, j, 2, g, half * s, half * (s + 1))
+                    mm_sorted(acc[:, 0:half], j, 2, g, half * s, half * (s + 1))
                 nc.scalar.copy(out=res[:, :, j, :], in_=acc[:, 0:half].rearrange("p (h d) -> p h d", h=hh))
-            store(nc.scalar, 2, 1, hh * s, hh * (s + 1), res)
+            store_sorted((nc.scalar, nc.sync), 2, hh * s, hh * (s + 1), res)

@@ -19,7 +19,7 @@ BLOCK = HEADS * HEAD_DIM
 FLOPS = 2 * TOKENS * 4096 * 3 * BLOCK
 
 K_SWEEP = 4
-WARM = 10
+WARM = 8
 
 
 def tile_attention_pa_kernel(tc, x_words, x_scales, rope, qkv_w_words, qkv_w_scales, out_0, out_1, out_2):
@@ -58,11 +58,6 @@ def tile_attention_pa_kernel(tc, x_words, x_scales, rope, qkv_w_words, qkv_w_sca
         nc.vector.memset(zeros[:], 0.0)
         xs_b = plane_tile("xs_b", 4, 0)
         qs_b = plane_tile("qs_b", 4, 0)
-        nc.gpsimd.dma_start(out=rope_sb[:, 0:2, :], in_=rope.rearrange("(u p) o d -> p u (o d)", u=2))
-        for b in range(2):
-            nc.gpsimd.dma_start(out=rope_sb[b:P:2, 2:6, :], in_=rope.rearrange("(q j) o d -> q j (o d)", j=4))
-        ks = plane_tile("ks", 8, 1)
-        vs = plane_tile("vs", 8, 1)
         nc.scalar.copy(out=tiny[:], in_=zeros[:, 0:8])
 
         def load_x(g0, g1):
@@ -99,21 +94,32 @@ def tile_attention_pa_kernel(tc, x_words, x_scales, rope, qkv_w_words, qkv_w_sca
 
         load_x(0, 1)
         load_w(0, 0, 1)
+        nc.gpsimd.dma_start(out=rope_sb[:, 0:2, :], in_=rope.rearrange("(u p) o d -> p u (o d)", u=2))
+        for b in range(2):
+            nc.gpsimd.dma_start(out=rope_sb[b:P:2, 2:6, :], in_=rope.rearrange("(q j) o d -> q j (o d)", j=4))
+        ks_a = plane_tile("ks_a", 4, 1)
+        ks_b = plane_tile("ks_b", 4, 1)
+        vs = plane_tile("vs", 8, 1)
         load_xs(xs_a, 0, 4)
         load_ws(qs_a, 0, 0, 4)
         load_x(1, 2)
         load_w(0, 1, 2)
-        load_x(2, 4)
-        load_w(0, 2, 4)
+        load_x(2, 3)
+        load_w(0, 2, 3)
         load_xs(xs_b, 4, 8)
+        load_x(3, 4)
+        load_w(0, 3, 4)
         load_ws(qs_b, 0, 4, 8)
-        load_x(4, 6)
-        load_w(0, 4, 6)
+        load_x(4, 5)
+        load_w(0, 4, 5)
+        load_x(5, 6)
+        load_w(0, 5, 6)
         load_x(6, 8)
         load_w(0, 6, 8)
-        load_ws(ks, 1, 0, 8)
+        load_ws(ks_a, 1, 0, 4)
         load_w(1, 0, 2)
         load_w(1, 2, 4)
+        load_ws(ks_b, 1, 4, 8)
         load_w(1, 4, 8)
         load_ws(vs, 2, 0, 8)
         load_w(2, 0, 4)

@@ -46,7 +46,7 @@ def tile_attention_pa_kernel(tc, x_words, x_scales, rope, qkv_w_words, qkv_w_sca
         wp_of = {}
 
         def plane_tile(name, n, engine):
-            t = keep.tile([P, n, BLOCK], U8, name=name, align_bytes=64)
+            t = keep.tile([P, n, BLOCK], U8, name=name, align_bytes=256)
             if engine == 0:
                 nc.vector.memset(t[:].bitcast(I32), 0)
             else:
@@ -61,13 +61,13 @@ def tile_attention_pa_kernel(tc, x_words, x_scales, rope, qkv_w_words, qkv_w_sca
         nc.scalar.copy(out=tiny[:], in_=zeros[:, 0:8])
 
         def load_x(g0, g1):
-            t = keep.tile([P, g1 - g0, 2 * TOKENS], U8, name="x_raw%d" % g0, align_bytes=64)
+            t = keep.tile([P, g1 - g0, 2 * TOKENS], U8, name="x_raw%d" % g0, align_bytes=256)
             nc.sync.dma_start(out=t[:].bitcast(I32), in_=x_words[g0:g1].rearrange("g p n -> p g n").bitcast(I32))
             for g in range(g0, g1):
                 raw_of[g] = t[:, g - g0, :]
 
         def load_w(c, g0, g1):
-            t = keep.tile([P, g1 - g0, 2 * BLOCK], U8, name="w_codes%d_%d" % (c, g0), align_bytes=64)
+            t = keep.tile([P, g1 - g0, 2 * BLOCK], U8, name="w_codes%d_%d" % (c, g0), align_bytes=256)
             nc.sync.dma_start(
                 out=t[:].bitcast(I32),
                 in_=qkv_w_words[g0:g1, :, 2 * BLOCK * c : 2 * BLOCK * (c + 1)].rearrange("g p n -> p g n").bitcast(I32),
@@ -126,7 +126,7 @@ def tile_attention_pa_kernel(tc, x_words, x_scales, rope, qkv_w_words, qkv_w_sca
         load_w(2, 4, 8)
 
         def sort_codes(g):
-            t = keep.tile([P, 2 * TOKENS], U8, name="x_codes%d" % g, align_bytes=64)
+            t = keep.tile([P, 2 * TOKENS], U8, name="x_codes%d" % g, align_bytes=256)
             nc.vector.tensor_copy(
                 out=t[:].rearrange("p (j q b e) -> p j q b e", j=4, b=2, e=2),
                 in_=raw_of[g].rearrange("p (b q j e) -> p j q b e", b=2, j=4, e=2),
@@ -134,7 +134,7 @@ def tile_attention_pa_kernel(tc, x_words, x_scales, rope, qkv_w_words, qkv_w_sca
             x_of[g] = t
 
         def sort_plane(g):
-            t = keep.tile([P, TOKENS], U8, name="x_plane%d" % g, align_bytes=64)
+            t = keep.tile([P, TOKENS], U8, name="x_plane%d" % g, align_bytes=256)
             nc.vector.tensor_copy(
                 out=t[:].rearrange("p (j q b) -> p j q b", j=4, b=2),
                 in_=rawp_of[g].rearrange("p (b q j) -> p j q b", b=2, j=4),
@@ -199,7 +199,7 @@ def tile_attention_pa_kernel(tc, x_words, x_scales, rope, qkv_w_words, qkv_w_sca
                     in_=res[b:P:2, :, :, :].rearrange("p h j d -> p h (j d)"),
                 )
 
-        res_k = keep.tile([P, HEADS, 4, HEAD_DIM], F32, name="res_k")
+        res_k = keep.tile([P, HEADS, 4, HEAD_DIM], F32, name="res_k", align_bytes=256)
         parts = {}
 
         def rope_mul(n):
@@ -218,7 +218,7 @@ def tile_attention_pa_kernel(tc, x_words, x_scales, rope, qkv_w_words, qkv_w_sca
         def rope_add(n):
             t1, t2 = parts[n]
             if n < 4:
-                res = keep.tile([P, HEADS, HEAD_DIM], F32, name="res_q%d" % n)
+                res = keep.tile([P, HEADS, HEAD_DIM], F32, name="res_q%d" % n, align_bytes=256)
                 dst = res[:]
             else:
                 dst = res_k[:, :, n - 4, :]
@@ -242,7 +242,7 @@ def tile_attention_pa_kernel(tc, x_words, x_scales, rope, qkv_w_words, qkv_w_sca
         half = BLOCK // 2
         hh = HEADS // 2
         for s in range(2):
-            res = keep.tile([P, hh, 4, HEAD_DIM], F32, name="res_v%d" % s)
+            res = keep.tile([P, hh, 4, HEAD_DIM], F32, name="res_v%d" % s, align_bytes=256)
             for j in range(4):
                 acc = psum.tile([P, BLOCK], F32, name="acc_v%d%d" % (s, j), tag="acc")
                 for g in range(PASSES):

@@ -34,9 +34,9 @@ def tile_attention_pa_kernel(tc, x_words, x_scales, rope, qkv_w_words, qkv_w_sca
 
         zeros = keep.tile([P, BLOCK], BF16, name="zeros")
         tiny = keep.tile([P, 8], F32, name="tiny")
-        rope_sb = keep.tile([P, 6, HEAD_DIM], BF16, name="rope_sb")
-        cos_t = keep.tile([P, 6, HEAD_DIM], F32, name="cos_t")
-        sin_t = keep.tile([P, 6, HEAD_DIM], F32, name="sin_t")
+        rope_sb = keep.tile([P, 4, HEAD_DIM], BF16, name="rope_sb")
+        cos_t = keep.tile([P, 4, HEAD_DIM], F32, name="cos_t")
+        sin_t = keep.tile([P, 4, HEAD_DIM], F32, name="sin_t")
 
         raw_of = {}
         rawp_of = {}
@@ -95,8 +95,7 @@ def tile_attention_pa_kernel(tc, x_words, x_scales, rope, qkv_w_words, qkv_w_sca
         load_x(0, 1)
         load_w(0, 0, 1)
         nc.gpsimd.dma_start(out=rope_sb[:, 0:2, :], in_=rope.rearrange("(u p) o d -> p u (o d)", u=2))
-        for b in range(2):
-            nc.gpsimd.dma_start(out=rope_sb[b:P:2, 2:6, :], in_=rope.rearrange("(q j) o d -> q j (o d)", j=4))
+        nc.gpsimd.dma_start(out=rope_sb[:, 2:4, :], in_=rope.rearrange("(m j) o d -> m j (o d)", j=2))
         ks_a = plane_tile("ks_a", 4, 1)
         ks_b = plane_tile("ks_b", 4, 1)
         vs = plane_tile("vs", 8, 1)
@@ -128,16 +127,16 @@ def tile_attention_pa_kernel(tc, x_words, x_scales, rope, qkv_w_words, qkv_w_sca
         def sort_codes(g):
             t = keep.tile([P, 2 * TOKENS], U8, name="x_codes%d" % g, align_bytes=256)
             nc.vector.tensor_copy(
-                out=t[:].rearrange("p (j q b e) -> p j q b e", j=4, b=2, e=2),
-                in_=raw_of[g].rearrange("p (b q j e) -> p j q b e", b=2, j=4, e=2),
+                out=t[:].rearrange("p (b j m e) -> p b j m e", b=2, j=2, e=2),
+                in_=raw_of[g].rearrange("p (b m j e) -> p b j m e", b=2, j=2, e=2),
             )
             x_of[g] = t
 
         def sort_plane(g):
             t = keep.tile([P, TOKENS], U8, name="x_plane%d" % g, align_bytes=256)
             nc.vector.tensor_copy(
-                out=t[:].rearrange("p (j q b) -> p j q b", j=4, b=2),
-                in_=rawp_of[g].rearrange("p (b q j) -> p j q b", b=2, j=4),
+                out=t[:].rearrange("p (b j m) -> p b j m", b=2, j=2),
+                in_=rawp_of[g].rearrange("p (b m j) -> p b j m", b=2, j=2),
             )
             xp_of[g] = t
 
@@ -192,18 +191,20 @@ def tile_attention_pa_kernel(tc, x_words, x_scales, rope, qkv_w_words, qkv_w_sca
             for g in range(K_SWEEP, PASSES):
                 mm_sorted(k_banks[j][:], j, 1, g, 0, BLOCK)
 
-        def store_sorted(queues, c, h0, h1, res):
-            for b in range(2):
-                queues[b].dma_start(
-                    out=outs[c][b, h0:h1, :, :].rearrange("h (q j) d -> q h (j d)", j=4),
-                    in_=res[b:P:2, :, :, :].rearrange("p h j d -> p h (j d)"),
-                )
+        def store_sorted(queue, c, b, h0, h1, res):
+            queue.dma_start(
+                out=outs[c][b, h0:h1, :, :].rearrange("h (m j) d -> m h (j d)", j=2),
+                in_=res[:].rearrange("p h j d -> p h (j d)"),
+            )
 
-        res_k = keep.tile([P, HEADS, 4, HEAD_DIM], F32, name="res_k", align_bytes=256)
+        res_k = []
+        for b in range(2):
+            res = keep.tile([P, HEADS, 2, HEAD_DIM], F32, name="res_k%d" % b, align_bytes=256)
+            res_k.append(res)
         parts = {}
 
         def rope_mul(n):
-            acc, slot = (q_banks[n], n % 2) if n < 4 else (k_banks[n - 4], n - 2)
+            acc, slot = (q_banks[n], n % 2) if n < 4 else (k_banks[n - 4], 2 + n % 2)
             t1 = work.tile([P, BLOCK], F32, name="t1", tag="t1")
             t2 = work.tile([P, BLOCK], F32, name="t2", tag="t2")
             acc_v = acc[:].rearrange("p (h d) -> p h d", h=HEADS)
@@ -221,7 +222,7 @@ def tile_attention_pa_kernel(tc, x_words, x_scales, rope, qkv_w_words, qkv_w_sca
                 res = keep.tile([P, HEADS, HEAD_DIM], F32, name="res_q%d" % n, align_bytes=256)
                 dst = res[:]
             else:
-                dst = res_k[:, :, n - 4, :]
+                dst = res_k[(n - 4) // 2][:, :, n % 2, :]
             nc.vector.tensor_tensor(
                 out=dst.rearrange("p h (x t) -> p h x t", t=2),
                 in0=t1[:].rearrange("p (h x t) -> p h x t", h=HEADS, t=2),
@@ -230,8 +231,8 @@ def tile_attention_pa_kernel(tc, x_words, x_scales, rope, qkv_w_words, qkv_w_sca
             if n < 4:
                 b, u = divmod(n, 2)
                 nc.sync.dma_start(out=outs[0][b, :, P * u : P * (u + 1), :].rearrange("h p d -> p h d"), in_=res[:])
-            if n == 7:
-                store_sorted((nc.sync, nc.sync), 1, 0, HEADS, res_k)
+            if n in (5, 7):
+                store_sorted(nc.sync, 1, (n - 4) // 2, 0, HEADS, res_k[(n - 4) // 2])
 
         rope_mul(0)
         for n in range(1, 8):
@@ -242,10 +243,11 @@ def tile_attention_pa_kernel(tc, x_words, x_scales, rope, qkv_w_words, qkv_w_sca
         half = BLOCK // 2
         hh = HEADS // 2
         for s in range(2):
-            res = keep.tile([P, hh, 4, HEAD_DIM], F32, name="res_v%d" % s, align_bytes=256)
-            for j in range(4):
-                acc = psum.tile([P, BLOCK], F32, name="acc_v%d%d" % (s, j), tag="acc")
-                for g in range(PASSES):
-                    mm_sorted(acc[:, 0:half], j, 2, g, half * s, half * (s + 1))
-                nc.scalar.copy(out=res[:, :, j, :], in_=acc[:, 0:half].rearrange("p (h d) -> p h d", h=hh))
-            store_sorted((nc.scalar, nc.sync), 2, hh * s, hh * (s + 1), res)
+            for b in range(2):
+                res = keep.tile([P, hh, 2, HEAD_DIM], F32, name="res_v%d%d" % (s, b), align_bytes=256)
+                for j in range(2):
+                    acc = psum.tile([P, BLOCK], F32, name="acc_v%d%d%d" % (s, b, j), tag="acc")
+                    for g in range(PASSES):
+                        mm_sorted(acc[:, 0:half], 2 * b + j, 2, g, half * s, half * (s + 1))
+                    nc.scalar.copy(out=res[:, :, j, :], in_=acc[:, 0:half].rearrange("p (h d) -> p h d", h=hh))
+                store_sorted(nc.scalar, 2, b, hh * s, hh * (s + 1), res)

@@ -19,7 +19,7 @@ BLOCK = HEADS * HEAD_DIM
 FLOPS = 2 * TOKENS * 4096 * 3 * BLOCK
 
 K_SWEEP = 4
-WARM = 8
+WARM = 6
 
 
 def tile_attention_pa_kernel(tc, x_words, x_scales, rope, qkv_w_words, qkv_w_scales, out_0, out_1, out_2):

@@ -94,8 +94,6 @@ def tile_attention_pa_kernel(tc, x_words, x_scales, rope, qkv_w_words, qkv_w_sca
 
         load_x(0, 1)
         load_w(0, 0, 1)
-        nc.gpsimd.dma_start(out=rope_sb[:, 0:2, :], in_=rope.rearrange("(u p) o d -> p u (o d)", u=2))
-        nc.gpsimd.dma_start(out=rope_sb[:, 2:4, :], in_=rope.rearrange("(m j) o d -> m j (o d)", j=2))
         ks_a = plane_tile("ks_a", 4, 1)
         ks_b = plane_tile("ks_b", 4, 1)
         vs = plane_tile("vs", 8, 1)
@@ -115,6 +113,8 @@ def tile_attention_pa_kernel(tc, x_words, x_scales, rope, qkv_w_words, qkv_w_sca
         load_w(0, 5, 6)
         load_x(6, 8)
         load_w(0, 6, 8)
+        nc.sync.dma_start(out=rope_sb[:, 0:2, :], in_=rope.rearrange("(u p) o d -> p u (o d)", u=2))
+        nc.sync.dma_start(out=rope_sb[:, 2:4, :], in_=rope.rearrange("(m j) o d -> m j (o d)", j=2))
         load_ws(ks_a, 1, 0, 4)
         load_w(1, 0, 2)
         load_w(1, 2, 4)

@@ -94,9 +94,6 @@ def tile_attention_pa_kernel(tc, x_words, x_scales, rope, qkv_w_words, qkv_w_sca
 
         load_x(0, 1)
         load_w(0, 0, 1)
-        ks_a = plane_tile("ks_a", 4, 1)
-        ks_b = plane_tile("ks_b", 4, 1)
-        vs = plane_tile("vs", 8, 1)
         load_xs(xs_a, 0, 4)
         load_ws(qs_a, 0, 0, 4)
         load_x(1, 2)
@@ -115,15 +112,6 @@ def tile_attention_pa_kernel(tc, x_words, x_scales, rope, qkv_w_words, qkv_w_sca
         load_w(0, 6, 8)
         nc.sync.dma_start(out=rope_sb[:, 0:2, :], in_=rope.rearrange("(u p) o d -> p u (o d)", u=2))
         nc.sync.dma_start(out=rope_sb[:, 2:4, :], in_=rope.rearrange("(m j) o d -> m j (o d)", j=2))
-        load_ws(ks_a, 1, 0, 4)
-        load_w(1, 0, 2)
-        load_w(1, 2, 4)
-        load_ws(ks_b, 1, 4, 8)
-        load_w(1, 4, 8)
-        load_ws(vs, 2, 0, 8)
-        load_w(2, 0, 4)
-        load_w(2, 4, 8)
-
         def sort_codes(g):
             t = keep.tile([P, 2 * TOKENS], U8, name="x_codes%d" % g, align_bytes=256)
             nc.vector.tensor_copy(
@@ -140,7 +128,20 @@ def tile_attention_pa_kernel(tc, x_words, x_scales, rope, qkv_w_words, qkv_w_sca
             )
             xp_of[g] = t
 
-        for g in range(PASSES):
+        sort_codes(0)
+        sort_plane(0)
+        ks_a = plane_tile("ks_a", 4, 0)
+        ks_b = plane_tile("ks_b", 4, 0)
+        vs = plane_tile("vs", 8, 0)
+        load_ws(ks_a, 1, 0, 4)
+        load_w(1, 0, 2)
+        load_w(1, 2, 4)
+        load_ws(ks_b, 1, 4, 8)
+        load_w(1, 4, 8)
+        load_ws(vs, 2, 0, 8)
+        load_w(2, 0, 4)
+        load_w(2, 4, 8)
+        for g in range(1, PASSES):
             sort_codes(g)
             sort_plane(g)
 

@@ -195,7 +195,7 @@ def tile_attention_pa_kernel(tc, x_words, x_scales, rope, qkv_w_words, qkv_w_sca
         def store_sorted(queue, c, b, h0, h1, res):
             queue.dma_start(
                 out=outs[c][b, h0:h1, :, :].rearrange("h (m j) d -> m h (j d)", j=2),
-                in_=res[:].rearrange("p h j d -> p h (j d)"),
+                in_=res[:, h0:h1, :, :].rearrange("p h j d -> p h (j d)"),
             )
 
         res_k = []
@@ -241,14 +241,21 @@ def tile_attention_pa_kernel(tc, x_words, x_scales, rope, qkv_w_words, qkv_w_sca
             rope_add(n - 1)
         rope_add(7)
 
-        half = BLOCK // 2
+        def v_group(res, b, j, h0, h1):
+            cols = (h1 - h0) * HEAD_DIM
+            acc = psum.tile([P, BLOCK], F32, name="acc_v%d%d_%d" % (b, j, h0), tag="acc")
+            for g in range(PASSES):
+                mm_sorted(acc[:, 0:cols], 2 * b + j, 2, g, HEAD_DIM * h0, HEAD_DIM * h1)
+            nc.scalar.copy(out=res[:, h0:h1, j, :], in_=acc[:, 0:cols].rearrange("p (h d) -> p h d", h=h1 - h0))
+
         hh = HEADS // 2
-        for s in range(2):
-            for b in range(2):
-                res = keep.tile([P, hh, 2, HEAD_DIM], F32, name="res_v%d%d" % (s, b), align_bytes=256)
-                for j in range(2):
-                    acc = psum.tile([P, BLOCK], F32, name="acc_v%d%d%d" % (s, b, j), tag="acc")
-                    for g in range(PASSES):
-                        mm_sorted(acc[:, 0:half], 2 * b + j, 2, g, half * s, half * (s + 1))
-                    nc.scalar.copy(out=res[:, :, j, :], in_=acc[:, 0:half].rearrange("p (h d) -> p h d", h=hh))
-                store_sorted(nc.scalar, 2, b, hh * s, hh * (s + 1), res)
+        res_v0 = keep.tile([P, HEADS, 2, HEAD_DIM], F32, name="res_v0", align_bytes=256)
+        res_v1 = keep.tile([P, HEADS, 2, HEAD_DIM], F32, name="res_v1", align_bytes=256)
+        v_group(res_v0, 0, 0, 0, HEADS)
+        v_group(res_v0, 0, 1, 0, HEADS)
+        store_sorted(nc.scalar, 2, 0, 0, HEADS, res_v0)
+        v_group(res_v1, 1, 0, 0, HEADS)
+        v_group(res_v1, 1, 1, 0, hh)
+        store_sorted(nc.scalar, 2, 1, 0, hh, res_v1)
+        v_group(res_v1, 1, 1, hh, HEADS)
+        store_sorted(nc.scalar, 2, 1, hh, HEADS, res_v1)

@@ -257,5 +257,7 @@ def tile_attention_pa_kernel(tc, x_words, x_scales, rope, qkv_w_words, qkv_w_sca
         v_group(res_v1, 1, 0, 0, HEADS)
         v_group(res_v1, 1, 1, 0, hh)
         store_sorted(nc.scalar, 2, 1, 0, hh, res_v1)
-        v_group(res_v1, 1, 1, hh, HEADS)
-        store_sorted(nc.scalar, 2, 1, hh, HEADS, res_v1)
+        v_group(res_v1, 1, 1, hh, hh + 4)
+        store_sorted(nc.scalar, 2, 1, hh, hh + 4, res_v1)
+        v_group(res_v1, 1, 1, hh + 4, HEADS)
+        store_sorted(nc.scalar, 2, 1, hh + 4, HEADS, res_v1)

@@ -148,10 +148,10 @@ def tile_attention_pa_kernel(tc, x_words, x_scales, rope, qkv_w_words, qkv_w_sca
         rope_v = rope_sb[:].rearrange("p u (i t) -> p (u i) t", t=2)
         cos_v = cos_t[:].rearrange("p u (i t) -> p (u i) t", t=2)
         sin_v = sin_t[:].rearrange("p u (i t) -> p (u i) t", t=2)
-        nc.gpsimd.tensor_copy(out=cos_v[:, :, 0:1], in_=rope_v[:, :, 0:1])
-        nc.gpsimd.tensor_copy(out=cos_v[:, :, 1:2], in_=rope_v[:, :, 0:1])
-        nc.gpsimd.tensor_copy(out=sin_v[:, :, 0:1], in_=rope_v[:, :, 1:2])
-        nc.gpsimd.tensor_scalar(out=sin_v[:, :, 1:2], in0=rope_v[:, :, 1:2], scalar1=-1.0, scalar2=0.0, op0=MULT, op1=ADD)
+        nc.scalar.copy(out=cos_v[:, :, 0:1], in_=rope_v[:, :, 0:1])
+        nc.scalar.copy(out=cos_v[:, :, 1:2], in_=rope_v[:, :, 0:1])
+        nc.scalar.copy(out=sin_v[:, :, 0:1], in_=rope_v[:, :, 1:2])
+        nc.scalar.mul(out=sin_v[:, :, 1:2], in_=rope_v[:, :, 1:2], mul=-1.0)
 
         warm = psum.tile([P, BLOCK], F32, name="warm", tag="acc")
         for n in range(WARM):

@@ -56,6 +56,7 @@ def tile_attention_pa_kernel(tc, x_words, x_scales, rope, qkv_w_words, qkv_w_sca
         xs_a = plane_tile("xs_a", 4, 0)
         qs_a = plane_tile("qs_a", 4, 0)
         nc.vector.memset(zeros[:], 0.0)
+        ks_a = plane_tile("ks_a", 4, 0)
         xs_b = plane_tile("xs_b", 4, 0)
         qs_b = plane_tile("qs_b", 4, 0)
         nc.scalar.copy(out=tiny[:], in_=zeros[:, 0:8])
@@ -100,14 +101,16 @@ def tile_attention_pa_kernel(tc, x_words, x_scales, rope, qkv_w_words, qkv_w_sca
         load_w(0, 1, 2)
         load_x(2, 3)
         load_w(0, 2, 3)
-        load_xs(xs_b, 4, 8)
+        load_w(1, 0, 1)
+        load_ws(ks_a, 1, 0, 4)
+        load_w(1, 1, 2)
         load_x(3, 4)
         load_w(0, 3, 4)
+        load_w(1, 2, 4)
+        load_xs(xs_b, 4, 8)
         load_ws(qs_b, 0, 4, 8)
-        load_x(4, 5)
-        load_w(0, 4, 5)
-        load_x(5, 6)
-        load_w(0, 5, 6)
+        load_x(4, 6)
+        load_w(0, 4, 6)
         load_x(6, 8)
         load_w(0, 6, 8)
         nc.sync.dma_start(out=rope_sb[:, 0:2, :], in_=rope.rearrange("(u p) o d -> p u (o d)", u=2))
@@ -130,12 +133,8 @@ def tile_attention_pa_kernel(tc, x_words, x_scales, rope, qkv_w_words, qkv_w_sca
 
         sort_codes(0)
         sort_plane(0)
-        ks_a = plane_tile("ks_a", 4, 0)
         ks_b = plane_tile("ks_b", 4, 0)
         vs = plane_tile("vs", 8, 0)
-        load_ws(ks_a, 1, 0, 4)
-        load_w(1, 0, 2)
-        load_w(1, 2, 4)
         load_ws(ks_b, 1, 4, 8)
         load_w(1, 4, 8)
         load_ws(vs, 2, 0, 8)
@@ -178,16 +177,30 @@ def tile_attention_pa_kernel(tc, x_words, x_scales, rope, qkv_w_words, qkv_w_sca
         for i in range(4):
             acc = psum.tile([P, BLOCK], F32, name="acc_q%d" % i, tag="acc")
             q_banks.append(acc)
-        for g in range(PASSES):
-            for i in range(4):
-                mm_plain(q_banks[i][:], i, 0, g)
         k_banks = []
         for j in range(4):
             acc = psum.tile([P, BLOCK], F32, name="acc_k%d" % j, tag="acc")
             k_banks.append(acc)
-        for g in range(K_SWEEP):
+
+        def q_sweep(g):
+            for i in range(4):
+                mm_plain(q_banks[i][:], i, 0, g)
+
+        def k_sweep(g):
             for j in range(4):
                 mm_sorted(k_banks[j][:], j, 1, g, 0, BLOCK)
+
+        q_sweep(0)
+        q_sweep(1)
+        q_sweep(2)
+        k_sweep(0)
+        k_sweep(1)
+        q_sweep(3)
+        k_sweep(2)
+        k_sweep(3)
+        for i in range(4):
+            for g in range(K_SWEEP, PASSES):
+                mm_plain(q_banks[i][:], i, 0, g)
         for j in range(4):
             for g in range(K_SWEEP, PASSES):
                 mm_sorted(k_banks[j][:], j, 1, g, 0, BLOCK)
@@ -224,7 +237,7 @@ def tile_attention_pa_kernel(tc, x_words, x_scales, rope, qkv_w_words, qkv_w_sca
                 dst = res[:]
             else:
                 dst = res_k[(n - 4) // 2][:, :, n % 2, :]
-            nc.vector.tensor_tensor(
+            nc.gpsimd.tensor_tensor(
                 out=dst.rearrange("p h (x t) -> p h x t", t=2),
                 in0=t1[:].rearrange("p (h x t) -> p h x t", h=HEADS, t=2),
                 in1=t2[:].rearrange("p (h x t) -> p h x t", h=HEADS, t=2)[:, :, :, ::-1],

@@ -93,10 +93,13 @@ def tile_attention_pa_kernel(tc, x_words, x_scales, rope, qkv_w_words, qkv_w_sca
             for g in range(g0, g1):
                 wp_of[(c, g)] = planes[:, g - g0, :]
 
-        load_x(0, 1)
+        x_raw0 = keep.tile([P, 2 * TOKENS], U8, name="x_raw0", align_bytes=256)
+        raw_of[0] = x_raw0[:, :]
         load_w(0, 0, 1)
+        nc.sync.dma_start(out=x_raw0[:, 0 : 2 * P].bitcast(I32), in_=x_words[0, :, 0 : 2 * P].bitcast(I32))
         load_xs(xs_a, 0, 4)
         load_ws(qs_a, 0, 0, 4)
+        nc.sync.dma_start(out=x_raw0[:, 2 * P : 2 * TOKENS].bitcast(I32), in_=x_words[0, :, 2 * P : 2 * TOKENS].bitcast(I32))
         load_x(1, 2)
         load_w(0, 1, 2)
         load_x(2, 3)

@@ -30,7 +30,6 @@ def tile_attention_pa_kernel(tc, x_words, x_scales, rope, qkv_w_words, qkv_w_sca
         keep = ctx.enter_context(tc.tile_pool(name="keep", bufs=1))
         work = ctx.enter_context(tc.tile_pool(name="work", bufs=3))
         psum = ctx.enter_context(tc.psum_pool(name="psum", bufs=8))
-        ctx.enter_context(tc.manual_schedule())
 
         zeros = keep.tile([P, BLOCK], BF16, name="zeros")
         tiny = keep.tile([P, 8], F32, name="tiny")

@@ -200,12 +200,14 @@ def tile_attention_pa_kernel(tc, x_words, x_scales, rope, qkv_w_words, qkv_w_sca
         q_sweep(3)
         k_sweep(2)
         k_sweep(3)
-        for i in range(4):
+        for i in (0, 2):
             for g in range(K_SWEEP, PASSES):
                 mm_plain(q_banks[i][:], i, 0, g)
-        for j in range(4):
+                mm_plain(q_banks[i + 1][:], i + 1, 0, g)
+        for j in (0, 2):
             for g in range(K_SWEEP, PASSES):
                 mm_sorted(k_banks[j][:], j, 1, g, 0, BLOCK)
+                mm_sorted(k_banks[j + 1][:], j + 1, 1, g, 0, BLOCK)
 
         def store_sorted(queue, c, b, h0, h1, res):
             queue.dma_start(
@@ -266,8 +268,13 @@ def tile_attention_pa_kernel(tc, x_words, x_scales, rope, qkv_w_words, qkv_w_sca
         hh = HEADS // 2
         res_v0 = keep.tile([P, HEADS, 2, HEAD_DIM], F32, name="res_v0", align_bytes=256)
         res_v1 = keep.tile([P, HEADS, 2, HEAD_DIM], F32, name="res_v1", align_bytes=256)
-        v_group(res_v0, 0, 0, 0, HEADS)
-        v_group(res_v0, 0, 1, 0, HEADS)
+        acc_v0 = psum.tile([P, BLOCK], F32, name="acc_v00", tag="acc")
+        acc_v1 = psum.tile([P, BLOCK], F32, name="acc_v01", tag="acc")
+        for g in range(PASSES):
+            mm_sorted(acc_v0[:], 0, 2, g, 0, BLOCK)
+            mm_sorted(acc_v1[:], 1, 2, g, 0, BLOCK)
+        nc.scalar.copy(out=res_v0[:, :, 0, :], in_=acc_v0[:].rearrange("p (h d) -> p h d", h=HEADS))
+        nc.scalar.copy(out=res_v0[:, :, 1, :], in_=acc_v1[:].rearrange("p (h d) -> p h d", h=HEADS))
         store_sorted(nc.scalar, 2, 0, 0, HEADS, res_v0)
         v_group(res_v1, 1, 0, 0, HEADS)
         v_group(res_v1, 1, 1, 0, hh)

@@ -19,7 +19,7 @@ BLOCK = HEADS * HEAD_DIM
 FLOPS = 2 * TOKENS * 4096 * 3 * BLOCK
 
 K_SWEEP = 4
-WARM = 6
+WARM = 8
 
 
 def tile_attention_pa_kernel(tc, x_words, x_scales, rope, qkv_w_words, qkv_w_scales, out_0, out_1, out_2):
@@ -31,7 +31,7 @@ def tile_attention_pa_kernel(tc, x_words, x_scales, rope, qkv_w_words, qkv_w_sca
         work = ctx.enter_context(tc.tile_pool(name="work", bufs=3))
         psum = ctx.enter_context(tc.psum_pool(name="psum", bufs=8))
 
-        zeros = keep.tile([P, BLOCK], BF16, name="zeros")
+        zeros = keep.tile([P, 8], BF16, name="zeros")
         tiny = keep.tile([P, 8], F32, name="tiny")
         rope_sb = keep.tile([P, 4, HEAD_DIM], BF16, name="rope_sb")
         cos_t = keep.tile([P, 4, HEAD_DIM], F32, name="cos_t")
@@ -52,9 +52,9 @@ def tile_attention_pa_kernel(tc, x_words, x_scales, rope, qkv_w_words, qkv_w_sca
                 nc.gpsimd.memset(t[:].bitcast(F32), 0.0)
             return t
 
+        nc.vector.memset(zeros[:], 0.0)
         xs_a = plane_tile("xs_a", 4, 0)
         qs_a = plane_tile("qs_a", 4, 0)
-        nc.vector.memset(zeros[:], 0.0)
         ks_a = plane_tile("ks_a", 4, 0)
         xs_b = plane_tile("xs_b", 4, 0)
         qs_b = plane_tile("qs_b", 4, 0)
@@ -156,7 +156,7 @@ def tile_attention_pa_kernel(tc, x_words, x_scales, rope, qkv_w_words, qkv_w_sca
 
         warm = psum.tile([P, BLOCK], F32, name="warm", tag="acc")
         for n in range(WARM):
-            nc.tensor.matmul(out=warm[:], lhsT=zeros[:, 0:P], rhs=zeros[:], start=True, stop=True)
+            nc.tensor.matmul(out=warm[:], lhsT=zeros[:, 0:1].to_broadcast([P, P]), rhs=zeros[:, 0:1].to_broadcast([P, BLOCK]), start=True, stop=True)
 
         def mm(acc, codes, plane, i, c, g, n0, n1):
             nc.tensor.matmul_mx(

@@ -276,9 +276,10 @@ def tile_attention_pa_kernel(tc, x_words, x_scales, rope, qkv_w_words, qkv_w_sca
         nc.scalar.copy(out=res_v0[:, :, 0, :], in_=acc_v0[:].rearrange("p (h d) -> p h d", h=HEADS))
         nc.scalar.copy(out=res_v0[:, :, 1, :], in_=acc_v1[:].rearrange("p (h d) -> p h d", h=HEADS))
         store_sorted(nc.scalar, 2, 0, 0, HEADS, res_v0)
-        v_group(res_v1, 1, 0, 0, HEADS)
+        v_group(res_v1, 1, 0, 0, hh)
         v_group(res_v1, 1, 1, 0, hh)
         store_sorted(nc.scalar, 2, 1, 0, hh, res_v1)
+        v_group(res_v1, 1, 0, hh, HEADS)
         v_group(res_v1, 1, 1, hh, hh + 4)
         store_sorted(nc.scalar, 2, 1, hh, hh + 4, res_v1)
         v_group(res_v1, 1, 1, hh + 4, HEADS)

from contextlib import ExitStack

import concourse.mybir as mybir

F32 = mybir.dt.float32
BF16 = mybir.dt.bfloat16
U8 = mybir.dt.uint8
I32 = mybir.dt.int32
FP4X4 = mybir.dt.float4_e2m1fn_x4
MULT = mybir.AluOpType.mult
ADD = mybir.AluOpType.add

P = 128
PASSES = 8
TOKENS = 512
HEADS = 16
HEAD_DIM = 32
BLOCK = HEADS * HEAD_DIM
FLOPS = 2 * TOKENS * 4096 * 3 * BLOCK

K_SWEEP = 4
WARM = 8


def tile_attention_pa_kernel(tc, x_words, x_scales, rope, qkv_w_words, qkv_w_scales, out_0, out_1, out_2):
    nc = tc.nc
    outs = (out_0, out_1, out_2)

    with ExitStack() as ctx:
        keep = ctx.enter_context(tc.tile_pool(name="keep", bufs=1))
        work = ctx.enter_context(tc.tile_pool(name="work", bufs=3))
        psum = ctx.enter_context(tc.psum_pool(name="psum", bufs=8))

        zeros = keep.tile([P, 8], BF16, name="zeros")
        tiny = keep.tile([P, 8], F32, name="tiny")
        rope_sb = keep.tile([P, 4, HEAD_DIM], BF16, name="rope_sb")
        cos_t = keep.tile([P, 4, HEAD_DIM], F32, name="cos_t")
        sin_t = keep.tile([P, 4, HEAD_DIM], F32, name="sin_t")

        raw_of = {}
        rawp_of = {}
        x_of = {}
        xp_of = {}
        w_of = {}
        wp_of = {}

        def plane_tile(name, n, engine):
            t = keep.tile([P, n, BLOCK], U8, name=name, align_bytes=256)
            if engine == 0:
                nc.vector.memset(t[:].bitcast(I32), 0)
            else:
                nc.gpsimd.memset(t[:].bitcast(F32), 0.0)
            return t

        nc.vector.memset(zeros[:], 0.0)
        xs_a = plane_tile("xs_a", 4, 0)
        qs_a = plane_tile("qs_a", 4, 0)
        ks_a = plane_tile("ks_a", 4, 0)
        xs_b = plane_tile("xs_b", 4, 0)
        qs_b = plane_tile("qs_b", 4, 0)
        nc.scalar.copy(out=tiny[:], in_=zeros[:, 0:8])

        def load_x(g0, g1):
            t = keep.tile([P, g1 - g0, 2 * TOKENS], U8, name="x_raw%d" % g0, align_bytes=256)
            nc.sync.dma_start(out=t[:].bitcast(I32), in_=x_words[g0:g1].rearrange("g p n -> p g n").bitcast(I32))
            for g in range(g0, g1):
                raw_of[g] = t[:, g - g0, :]

        def load_w(c, g0, g1):
            t = keep.tile([P, g1 - g0, 2 * BLOCK], U8, name="w_codes%d_%d" % (c, g0), align_bytes=256)
            nc.sync.dma_start(
                out=t[:].bitcast(I32),
                in_=qkv_w_words[g0:g1, :, 2 * BLOCK * c : 2 * BLOCK * (c + 1)].rearrange("g p n -> p g n").bitcast(I32),
            )
            for g in range(g0, g1):
                w_of[(c, g)] = t[:, g - g0, :]

        def load_planes(planes, scales, g0, g1):
            for r in range(4):
                nc.sync.dma_start(
                    out=planes[r:P:32, :, :].bitcast(I32),
                    in_=scales[g0:g1, r:16:4, :].rearrange("g q n -> q g n").bitcast(I32),
                )

        def load_xs(planes, g0, g1):
            load_planes(planes, x_scales, g0, g1)
            for g in range(g0, g1):
                rawp_of[g] = planes[:, g - g0, :]

        def load_ws(planes, c, g0, g1):
            load_planes(planes, qkv_w_scales[:, :, BLOCK * c : BLOCK * (c + 1)], g0, g1)
            for g in range(g0, g1):
                wp_of[(c, g)] = planes[:, g - g0, :]

        x_raw0 = keep.tile([P, 2 * TOKENS], U8, name="x_raw0", align_bytes=256)
        raw_of[0] = x_raw0[:, :]
        load_w(0, 0, 1)
        nc.sync.dma_start(out=x_raw0[:, 0 : 2 * P].bitcast(I32), in_=x_words[0, :, 0 : 2 * P].bitcast(I32))
        load_xs(xs_a, 0, 4)
        load_ws(qs_a, 0, 0, 4)
        nc.sync.dma_start(out=x_raw0[:, 2 * P : 2 * TOKENS].bitcast(I32), in_=x_words[0, :, 2 * P : 2 * TOKENS].bitcast(I32))
        load_x(1, 2)
        load_w(0, 1, 2)
        load_x(2, 3)
        load_w(0, 2, 3)
        load_w(1, 0, 1)
        load_ws(ks_a, 1, 0, 4)
        load_w(1, 1, 2)
        load_x(3, 4)
        load_w(0, 3, 4)
        load_w(1, 2, 4)
        load_xs(xs_b, 4, 8)
        load_ws(qs_b, 0, 4, 8)
        load_x(4, 6)
        load_w(0, 4, 6)
        load_x(6, 8)
        load_w(0, 6, 8)
        nc.sync.dma_start(out=rope_sb[:, 0:2, :], in_=rope.rearrange("(u p) o d -> p u (o d)", u=2))
        nc.sync.dma_start(out=rope_sb[:, 2:4, :], in_=rope.rearrange("(m j) o d -> m j (o d)", j=2))
        def sort_codes(g):
            t = keep.tile([P, 2 * TOKENS], U8, name="x_codes%d" % g, align_bytes=256)
            nc.vector.tensor_copy(
                out=t[:].rearrange("p (b j m e) -> p b j m e", b=2, j=2, e=2),
                in_=raw_of[g].rearrange("p (b m j e) -> p b j m e", b=2, j=2, e=2),
            )
            x_of[g] = t

        def sort_plane(g):
            t = keep.tile([P, TOKENS], U8, name="x_plane%d" % g, align_bytes=256)
            nc.vector.tensor_copy(
                out=t[:].rearrange("p (b j m) -> p b j m", b=2, j=2),
                in_=rawp_of[g].rearrange("p (b m j) -> p b j m", b=2, j=2),
            )
            xp_of[g] = t

        sort_codes(0)
        sort_plane(0)
        ks_b = plane_tile("ks_b", 4, 0)
        vs = plane_tile("vs", 8, 0)
        load_ws(ks_b, 1, 4, 8)
        load_w(1, 4, 8)
        load_ws(vs, 2, 0, 8)
        load_w(2, 0, 4)
        load_w(2, 4, 8)
        for g in range(1, PASSES):
            sort_codes(g)
            sort_plane(g)

        rope_v = rope_sb[:].rearrange("p u (i t) -> p (u i) t", t=2)
        cos_v = cos_t[:].rearrange("p u (i t) -> p (u i) t", t=2)
        sin_v = sin_t[:].rearrange("p u (i t) -> p (u i) t", t=2)
        nc.scalar.copy(out=cos_v[:, :, 0:1], in_=rope_v[:, :, 0:1])
        nc.scalar.copy(out=cos_v[:, :, 1:2], in_=rope_v[:, :, 0:1])
        nc.scalar.copy(out=sin_v[:, :, 0:1], in_=rope_v[:, :, 1:2])
        nc.scalar.mul(out=sin_v[:, :, 1:2], in_=rope_v[:, :, 1:2], mul=-1.0)

        warm = psum.tile([P, BLOCK], F32, name="warm", tag="acc")
        for n in range(WARM):
            nc.tensor.matmul(out=warm[:], lhsT=zeros[:, 0:1].to_broadcast([P, P]), rhs=zeros[:, 0:1].to_broadcast([P, BLOCK]), start=True, stop=True)

        def mm(acc, codes, plane, i, c, g, n0, n1):
            nc.tensor.matmul_mx(
                out=acc,
                lhsT=codes[:, 2 * P * i : 2 * P * (i + 1)].bitcast(FP4X4),
                lhsT_scale=plane[:, P * i : P * (i + 1)],
                rhs=w_of[(c, g)][:, 2 * n0 : 2 * n1].bitcast(FP4X4),
                rhs_scale=wp_of[(c, g)][:, n0:n1],
                start=(g == 0),
                stop=(g == PASSES - 1),
            )

        def mm_plain(acc, i, c, g):
            mm(acc, raw_of[g], rawp_of[g], i, c, g, 0, BLOCK)

        def mm_sorted(acc, j, c, g, n0, n1):
            mm(acc, x_of[g], xp_of[g], j, c, g, n0, n1)

        q_banks = []
        for i in range(4):
            acc = psum.tile([P, BLOCK], F32, name="acc_q%d" % i, tag="acc")
            q_banks.append(acc)
        k_banks = []
        for j in range(4):
            acc = psum.tile([P, BLOCK], F32, name="acc_k%d" % j, tag="acc")
            k_banks.append(acc)

        def q_sweep(g):
            for i in range(4):
                mm_plain(q_banks[i][:], i, 0, g)

        def k_sweep(g):
            for j in range(4):
                mm_sorted(k_banks[j][:], j, 1, g, 0, BLOCK)

        q_sweep(0)
        q_sweep(1)
        q_sweep(2)
        k_sweep(0)
        k_sweep(1)
        q_sweep(3)
        k_sweep(2)
        k_sweep(3)
        for i in (0, 2):
            for g in range(K_SWEEP, PASSES):
                mm_plain(q_banks[i][:], i, 0, g)
                mm_plain(q_banks[i + 1][:], i + 1, 0, g)
        for j in (0, 2):
            for g in range(K_SWEEP, PASSES):
                mm_sorted(k_banks[j][:], j, 1, g, 0, BLOCK)
                mm_sorted(k_banks[j + 1][:], j + 1, 1, g, 0, BLOCK)

        def store_sorted(queue, c, b, h0, h1, res):
            queue.dma_start(
                out=outs[c][b, h0:h1, :, :].rearrange("h (m j) d -> m h (j d)", j=2),
                in_=res[:, h0:h1, :, :].rearrange("p h j d -> p h (j d)"),
            )

        res_k = []
        for b in range(2):
            res = keep.tile([P, HEADS, 2, HEAD_DIM], F32, name="res_k%d" % b, align_bytes=256)
            res_k.append(res)
        parts = {}

        def rope_mul(n):
            acc, slot = (q_banks[n], n % 2) if n < 4 else (k_banks[n - 4], 2 + n % 2)
            t1 = work.tile([P, BLOCK], F32, name="t1", tag="t1")
            t2 = work.tile([P, BLOCK], F32, name="t2", tag="t2")
            acc_v = acc[:].rearrange("p (h d) -> p h d", h=HEADS)
            nc.vector.tensor_tensor(
                out=t1[:].rearrange("p (h d) -> p h d", h=HEADS), in0=acc_v,
                in1=cos_t[:, slot, :].unsqueeze(1).to_broadcast([P, HEADS, HEAD_DIM]), op=MULT)
            nc.vector.tensor_tensor(
                out=t2[:].rearrange("p (h d) -> p h d", h=HEADS), in0=acc_v,
                in1=sin_t[:, slot, :].unsqueeze(1).to_broadcast([P, HEADS, HEAD_DIM]), op=MULT)
            parts[n] = (t1, t2)

        def rope_add(n):
            t1, t2 = parts[n]
            if n < 4:
                res = keep.tile([P, HEADS, HEAD_DIM], F32, name="res_q%d" % n, align_bytes=256)
                dst = res[:]
            else:
                dst = res_k[(n - 4) // 2][:, :, n % 2, :]
            nc.gpsimd.tensor_tensor(
                out=dst.rearrange("p h (x t) -> p h x t", t=2),
                in0=t1[:].rearrange("p (h x t) -> p h x t", h=HEADS, t=2),
                in1=t2[:].rearrange("p (h x t) -> p h x t", h=HEADS, t=2)[:, :, :, ::-1],
                op=ADD)
            if n < 4:
                b, u = divmod(n, 2)
                nc.sync.dma_start(out=outs[0][b, :, P * u : P * (u + 1), :].rearrange("h p d -> p h d"), in_=res[:])
            if n in (5, 7):
                store_sorted(nc.sync, 1, (n - 4) // 2, 0, HEADS, res_k[(n - 4) // 2])

        rope_mul(0)
        for n in range(1, 8):
            rope_mul(n)
            rope_add(n - 1)
        rope_add(7)

        def v_group(res, b, j, h0, h1):
            cols = (h1 - h0) * HEAD_DIM
            acc = psum.tile([P, BLOCK], F32, name="acc_v%d%d_%d" % (b, j, h0), tag="acc")
            for g in range(PASSES):
                mm_sorted(acc[:, 0:cols], 2 * b + j, 2, g, HEAD_DIM * h0, HEAD_DIM * h1)
            nc.scalar.copy(out=res[:, h0:h1, j, :], in_=acc[:, 0:cols].rearrange("p (h d) -> p h d", h=h1 - h0))

        hh = HEADS // 2
        res_v0 = keep.tile([P, HEADS, 2, HEAD_DIM], F32, name="res_v0", align_bytes=256)
        res_v1 = keep.tile([P, HEADS, 2, HEAD_DIM], F32, name="res_v1", align_bytes=256)
        acc_v0 = psum.tile([P, BLOCK], F32, name="acc_v00", tag="acc")
        acc_v1 = psum.tile([P, BLOCK], F32, name="acc_v01", tag="acc")
        for g in range(PASSES):
            mm_sorted(acc_v0[:], 0, 2, g, 0, BLOCK)
            mm_sorted(acc_v1[:], 1, 2, g, 0, BLOCK)
        nc.scalar.copy(out=res_v0[:, :, 0, :], in_=acc_v0[:].rearrange("p (h d) -> p h d", h=HEADS))
        nc.scalar.copy(out=res_v0[:, :, 1, :], in_=acc_v1[:].rearrange("p (h d) -> p h d", h=HEADS))
        store_sorted(nc.scalar, 2, 0, 0, HEADS, res_v0)
        v_group(res_v1, 1, 0, 0, hh)
        v_group(res_v1, 1, 1, 0, hh)
        store_sorted(nc.scalar, 2, 1, 0, hh, res_v1)
        v_group(res_v1, 1, 0, hh, HEADS)
        v_group(res_v1, 1, 1, hh, hh + 4)
        store_sorted(nc.scalar, 2, 1, hh, hh + 4, res_v1)
        v_group(res_v1, 1, 1, hh + 4, HEADS)
        store_sorted(nc.scalar, 2, 1, hh + 4, HEADS, res_v1)
